import numpy as np
import ml_dtypes


def mxq(x, axis, fmt="e4m3"):
    dtype, down = {"e4m3": (ml_dtypes.float8_e4m3fn, 7), "e5m2": (ml_dtypes.float8_e5m2, 14)}[fmt]
    v = np.moveaxis(np.asarray(x, np.float32).astype(ml_dtypes.bfloat16).astype(np.float64), axis, -1)
    blocks = v.reshape(v.shape[:-1] + (-1, 32))
    amax = np.abs(blocks).max(-1, keepdims=True)
    byte = np.maximum(np.where(amax > 0, np.frexp(amax)[1] - 1 + 127, 0) - down, 1)
    scale = np.exp2(byte - 127.0)
    codes = (blocks / scale).astype(np.float32).astype(dtype).astype(np.float64)
    return np.moveaxis((codes * scale).reshape(v.shape), -1, axis)


WIDE = False


def mx_kscale(k):
    if not WIDE:
        return np.ones(k)
    levels = np.array([10, -10, 5, -5, 0])
    if k % 512:
        return np.exp2(np.random.permutation(np.resize(levels, k // 32))).repeat(32)
    a = np.empty((k // 512, 16))
    for p in range(k // 512):
        a[p, :8] = np.random.permutation(np.resize(levels, 8))
        for g in range(8):
            far = levels[np.abs(levels - a[p, g]) >= 10]
            a[p, g + 8] = far[np.random.randint(len(far))]
    return np.exp2(a.ravel()).repeat(32)


BF16 = ml_dtypes.bfloat16


def bf(x):
    return np.asarray(x, np.float32).astype(BF16)


def f64(x):
    return np.asarray(x).astype(np.float64)


B, H, NSE = 2048, 512, 1024


def sigmoid(v):
    return 1.0 / (1.0 + np.exp(-v))


def setup_inputs():
    s = mx_kscale(B)[:, None]
    e = np.frexp(mx_kscale(NSE))[1] - 1
    t = np.ldexp(1.0, e >> 1)
    u = t * t
    z_i0 = bf(np.random.standard_normal((B, H)))
    z_j = bf(np.random.standard_normal((B, H)))
    R = bf(np.eye(H) + np.random.standard_normal((H, H)) / np.sqrt(H))
    D0 = bf((1.0 + 0.3 * np.random.standard_normal((NSE, H))) * 0.9 / H ** 0.25)
    g = bf(np.random.standard_normal((B, NSE)) * np.exp2(np.random.randint(-6, 1, (B, 1))) * 4.0 / s * u[None, :])
    Rz = f64(z_j) @ f64(R).T
    scores = (f64(z_i0) * Rz) @ (f64(D0) * f64(D0)).T
    return {"z_i": bf(f64(z_i0) * s), "z_j": z_j, "R": R, "D": bf(f64(D0) / t[:, None]),
            "Rz": np.asarray(Rz, np.float32), "scores": np.asarray(scores, np.float32), "grad_out": g}


def reference(z_i, z_j, R, D, Rz, scores, grad_out):
    sg = sigmoid(f64(scores))
    dz = f64(grad_out) * (sg * (1.0 - sg))
    rz = f64(Rz)
    p = f64(z_i) * rz
    d = f64(D)
    d2 = d * d
    dp = mxq(dz, 1, "e5m2") @ mxq(d2, 0, "e4m3")
    dd2 = mxq(dz, 0, "e5m2").T @ mxq(p, 0, "e4m3")
    return dp * rz, 2.0 * d * dd2

@@ -1,0 +1,409 @@
+from contextlib import ExitStack
+
+import concourse.mybir as mybir
+from concourse.masks import make_identity
+
+B, H, R = 2048, 512, 1024
+
+FLOPS = 2 * 2 * B * H * R
+BYTES = 2 * B * H + 2 * R * H + 4 * B * H + 4 * B * R + 2 * B * R + 4 * B * H + 4 * R * H
+
+F32 = mybir.dt.float32
+BF16 = mybir.dt.bfloat16
+U32 = mybir.dt.uint32
+U8 = mybir.dt.uint8
+E4M3 = mybir.dt.float8_e4m3fn_x4
+E5M2 = mybir.dt.float8_e5m2_x4
+ACT = mybir.ActivationFunctionType
+ALU = mybir.AluOpType
+
+P = 128
+NT = B // 512
+NG = R // 512
+NU = NT * NG
+
+
+def tile_dedicomdecoder_v_kernel(tc, z_i, z_j, w_r, d_w, rz_in, scores, grad_out, out_0, out_1):
+    nc = tc.nc
+    with ExitStack() as ctx:
+        keep = ctx.enter_context(tc.tile_pool(name="keep", bufs=1))
+        s_pool = ctx.enter_context(tc.tile_pool(name="s_pool", bufs=5))
+        three = ctx.enter_context(tc.tile_pool(name="three", bufs=3))
+        two = ctx.enter_context(tc.tile_pool(name="two", bufs=2))
+        ps_wk = ctx.enter_context(tc.psum_pool(name="ps_wk", bufs=2))
+        ps_o0 = ctx.enter_context(tc.psum_pool(name="ps_o0", bufs=2))
+        ps_acc = ctx.enter_context(tc.psum_pool(name="ps_acc", bufs=1))
+        ctx.enter_context(tc.manual_schedule())
+
+        s_t, g_t, z_t, rz_t = {}, {}, {}, {}
+
+        def load_s(u, pieces=1):
+            t, g = divmod(u, NG)
+            tile = s_pool.tile([P, 4, 512], F32, name="s_tile")
+            src = scores[512 * t : 512 * (t + 1), 512 * g : 512 * (g + 1)].rearrange("(p j) n -> p j n", j=4)
+            w = 4 // pieces
+            for i in range(pieces):
+                nc.sync.dma_start(out=tile[:, w * i : w * (i + 1), :], in_=src[:, w * i : w * (i + 1), :])
+                if i == 0 and u == 0:
+                    load_d(0)
+            s_t[u] = tile
+
+        def load_d(g):
+            nc.sync.dma_start(
+                out=d_sb[:, g, :, :], in_=d_w[512 * g : 512 * (g + 1), :].rearrange("(p j) h -> p j h", j=4)
+            )
+
+        def load_g(t):
+            tile = three.tile([P, 4, R], BF16, name="g_tile")
+            src = grad_out[512 * t : 512 * (t + 1), :].rearrange("(p j) n -> p j n", j=4)
+            g_t[t] = tile
+            if t == 0:
+                nc.sync.dma_start(out=tile[:, :, 0:512], in_=src[:, :, 0:512])
+            else:
+                nc.sync.dma_start(out=tile[:], in_=src)
+
+        def load_g0b():
+            src = grad_out[0:512, :].rearrange("(p j) n -> p j n", j=4)
+            nc.sync.dma_start(out=g_t[0][:, :, 512:1024], in_=src[:, :, 512:1024])
+
+        def load_p(t):
+            tile = two.tile([P, 4, H], BF16, name="z_tile")
+            nc.sync.dma_start(out=tile[:], in_=z_i[512 * t : 512 * (t + 1), :].rearrange("(p j) n -> p j n", j=4))
+            z_t[t] = tile
+            tile2 = keep.tile([P, 4, H], F32, name="rz_tile%d" % t)
+            nc.sync.dma_start(out=tile2[:], in_=rz_in[512 * t : 512 * (t + 1), :].rearrange("(p j) n -> p j n", j=4))
+            rz_t[t] = tile2
+
+        ident = keep.tile([P, P], F32, name="ident")
+        make_identity(nc, ident[:])
+        ident_b = keep.tile([P, P], BF16, name="ident_b")
+        make_identity(nc, ident_b[:])
+        warm = keep.tile([P, 1], F32, name="warm")
+        nc.vector.memset(warm[:], 0.0)
+        warm2 = keep.tile([P, 1], F32, name="warm2")
+        nc.scalar.activation(out=warm2[:], in_=warm[:], func=ACT.Tanh)
+
+        d_sb = keep.tile([P, NG, 4, H], BF16, name="d_sb")
+        load_s(0, pieces=4)
+        load_g(0)
+        load_s(1)
+        load_d(1)
+        load_g0b()
+        load_s(2)
+        load_p(0)
+        load_g(1)
+        load_s(3)
+        load_s(4)
+        load_p(1)
+        load_g(2)
+
+        d2_code = keep.tile([P, NG, H], U32, name="d2_code", align_bytes=64)
+        d2_scale = keep.tile([P, NG, H], U8, name="d2_scale", align_bytes=64)
+        p_code = keep.tile([P, NT, H], U32, name="p_code", align_bytes=64)
+        p_scale = keep.tile([P, NT, H], U8, name="p_scale", align_bytes=64)
+        t_code = keep.tile([P, NT + 2, 512], U32, name="t_code", align_bytes=64)
+        t_scale = keep.tile([P, NT + 2, 512], U8, name="t_scale", align_bytes=64)
+        r_code = keep.tile([P, 4, 512], U32, name="r_code", align_bytes=64)
+        r_scale = keep.tile([P, 4, 512], U8, name="r_scale", align_bytes=64)
+
+        def act(u, func, j0, j1):
+            s = s_t[u][:, j0:j1, :]
+            nc.scalar.activation(out=s, in_=s, func=func, scale=0.5)
+
+        dz_t, dzi_t, dzr_t, p_t, tr_t = {}, {}, {}, {}, {}
+
+        def slot(u):
+            t, g = divmod(u, NG)
+            return t if g == 1 else NT + t % 2
+
+        def stt(u, j0=0, j1=4):
+            t, g = divmod(u, NG)
+            if j0 == 0:
+                dz_t[u] = three.tile([P, 4, 512], BF16, name="dz", align_bytes=64)
+            j = slice(j0, j1)
+            nc.vector.scalar_tensor_tensor(
+                out=dz_t[u][:, j, :],
+                in0=s_t[u][:, j, :],
+                scalar=0.25,
+                in1=g_t[t][:, j, 512 * g : 512 * (g + 1)],
+                op0=ALU.subtract,
+                op1=ALU.mult,
+            )
+
+        il_bank = {}
+
+        def il_pe(u, r0, r1):
+            if u not in dzi_t:
+                dzi_t[u] = two.tile([P, 4, P, 4], BF16, name="dzi", align_bytes=64)
+            src = dz_t[u][:].rearrange("p t (m r) -> p r m t", r=4)
+            bank = ps_wk.tile([P, r1 - r0, P, 4], BF16, name="bank")
+            for r in range(r0, r1):
+                nc.tensor.matmul(bank[:, r - r0, :, :], lhsT=ident_b[:], rhs=src[:, r, :, :], start=True, stop=True)
+            il_bank[u, r0] = bank
+
+        def il_cp(u, r0, r1):
+            nc.scalar.copy(out=dzi_t[u][:, r0:r1, :, :], in_=il_bank[u, r0][:])
+
+        def il(u, r0, r1, eng):
+            if r0 == r1:
+                return
+            if u not in dzi_t:
+                dzi_t[u] = two.tile([P, 4, P, 4], BF16, name="dzi", align_bytes=64)
+            dst = dzi_t[u][:, r0:r1, :, :].rearrange("p r m t -> p m t r")
+            src = dz_t[u][:].rearrange("p t (m r) -> p m t r", r=4)[:, :, :, r0:r1]
+            if eng == "s":
+                nc.scalar.copy(out=dst, in_=src)
+            else:
+                nc.vector.tensor_copy(out=dst, in_=src)
+
+        def q_t(u):
+            nc.vector.quantize_mx(
+                out=t_code[:, slot(u), :].bitcast(E5M2),
+                scales=t_scale[:, slot(u), :],
+                in_=dzi_t[u][:].rearrange("p r m t -> p (r m t)"),
+            )
+
+        def tr(u, b):
+            words = dz_t[u][:].rearrange("p j n -> p (j n)").bitcast(F32)
+            bank = ps_wk.tile([P, 2, 2, P], F32, name="bank")
+            for jj in range(2):
+                w0 = 256 * (2 * b + jj)
+                for h in range(2):
+                    nc.tensor.transpose(bank[:, jj, h, :], words[:, w0 + h : w0 + 256 : 2], ident[:])
+            tr_t[u, b] = bank
+            if b == 0:
+                dzr_t[u] = two.tile([P, 4, P, 4], BF16, name="dzr", align_bytes=64)
+
+        def cp(u, b, eng):
+            src = tr_t[u, b][:].rearrange("m j h p -> m j p h")
+            dst = dzr_t[u][:].rearrange("m j p r -> m (j p r)").bitcast(F32)[:, 512 * b : 512 * (b + 1)]
+            dst = dst.rearrange("m (j p h) -> m j p h", j=2, h=2)
+            if eng == "s":
+                nc.scalar.copy(out=dst, in_=src)
+            else:
+                nc.vector.tensor_copy(out=dst, in_=src)
+
+        def q_r(u, j0=0, j1=4):
+            nc.vector.quantize_mx(
+                out=r_code[:, u % 4, P * j0 : P * j1].bitcast(E5M2),
+                scales=r_scale[:, u % 4, P * j0 : P * j1],
+                in_=dzr_t[u][:, j0:j1, :, :].rearrange("m j p r -> m (j p r)"),
+            )
+
+        def make_p(t, half):
+            if half == 0:
+                p_t[t] = two.tile([P, H, 4], BF16, name="p_tile", align_bytes=64)
+            cols = slice(256 * half, 256 * (half + 1))
+            nc.vector.tensor_tensor(
+                out=p_t[t][:, cols, :].rearrange("p (c i) t -> p c t i", i=4),
+                in0=z_t[t][:, :, cols].rearrange("p t (c i) -> p c t i", i=4),
+                in1=rz_t[t][:, :, cols].rearrange("p t (c i) -> p c t i", i=4),
+                op=ALU.mult,
+            )
+
+        def q_p(t):
+            nc.vector.quantize_mx(
+                out=p_code[:, t, :].bitcast(E4M3),
+                scales=p_scale[:, t, :],
+                in_=p_t[t][:].rearrange("p h t -> p (h t)"),
+            )
+
+        d2_t = {}
+
+        def make_d2(g, eng="v"):
+            d2 = two.tile([P, H, 4], BF16, name="d2", align_bytes=64)
+            v = d_sb[:, g, :, :].rearrange("p t (c i) -> p c t i", i=4)
+            if eng == "s":
+                nc.scalar.activation(out=d2[:].rearrange("p (c i) t -> p c t i", i=4), in_=v, func=ACT.Square)
+            else:
+                nc.vector.tensor_tensor(out=d2[:].rearrange("p (c i) t -> p c t i", i=4), in0=v, in1=v, op=ALU.mult)
+            d2_t[g] = d2
+
+        def q_d(g):
+            nc.vector.quantize_mx(
+                out=d2_code[:, g, :].bitcast(E4M3),
+                scales=d2_scale[:, g, :],
+                in_=d2_t[g][:].rearrange("p h t -> p (h t)"),
+            )
+
+        o0_t, o0_bank = {}, {}
+
+        def mm0(t, j, spare=False):
+            if spare:
+                bank = ps_wk.tile([P, H], F32, name="bank")
+            else:
+                bank = ps_o0.tile([P, H], F32, name="o0_bank_tile")
+            for g in range(NG):
+                u = NG * t + g
+                nc.tensor.matmul_mx(
+                    out=bank[:],
+                    lhsT=r_code[:, u % 4, P * j : P * (j + 1)].bitcast(E5M2),
+                    lhsT_scale=r_scale[:, u % 4, P * j : P * (j + 1)],
+                    rhs=d2_code[:, g, :].bitcast(E4M3),
+                    rhs_scale=d2_scale[:, g, :],
+                    start=(g == 0),
+                    stop=(g == NG - 1),
+                )
+            o0_bank[t, j] = bank
+
+        def ev0(t, j):
+            if j == 0:
+                o0_t[t] = two.tile([P, 4, H], F32, name="o0_tile")
+            nc.vector.scalar_tensor_tensor(
+                out=o0_t[t][:, j, :], in0=o0_bank[t, j][:], scalar=-1.0, in1=rz_t[t][:, j, :], op0=ALU.mult, op1=ALU.mult
+            )
+
+        def st0(t, j0, j1):
+            dst = out_0[512 * t : 512 * (t + 1), :].rearrange("(p j) h -> p j h", j=4)
+            nc.sync.dma_start(out=dst[:, j0:j1, :], in_=o0_t[t][:, j0:j1, :])
+
+        acc = {}
+
+        def mm1(t, g):
+            u = NG * t + g
+            for r in range(4):
+                if t == 0:
+                    acc[g, r] = ps_acc.tile([P, H], F32, name="acc%d" % r)
+                nc.tensor.matmul_mx(
+                    out=acc[g, r][:],
+                    lhsT=t_code[:, slot(u), P * r : P * (r + 1)].bitcast(E5M2),
+                    lhsT_scale=t_scale[:, slot(u), P * r : P * (r + 1)],
+                    rhs=p_code[:, t, :].bitcast(E4M3),
+                    rhs_scale=p_scale[:, t, :],
+                    start=(t == 0),
+                    stop=(t == NT - 1),
+                )
+
+        o1_t = {}
+
+        def ev1(g, r):
+            if r == 0:
+                o1_t[g] = two.tile([P, 4, H], F32, name="o1_tile")
+            nc.vector.scalar_tensor_tensor(
+                out=o1_t[g][:, r, :], in0=acc[g, r][:], scalar=-2.0, in1=d_sb[:, g, r, :], op0=ALU.mult, op1=ALU.mult
+            )
+
+        def st1(g, r0, r1):
+            dst = out_1[512 * g : 512 * (g + 1), :].rearrange("(m r) h -> m r h", r=4)
+            nc.sync.dma_start(out=dst[:, r0:r1, :], in_=o1_t[g][:, r0:r1, :])
+
+        blocks = {0: ([], [(0, 4)], [])}
+        for u in range(1, NU):
+            blocks[u] = ([(0, 2), (2, 3)], [(3, 4)], [])
+        make_d2(0)
+        for jj in range(4):
+            act(0, ACT.Tanh, jj, jj + 1)
+            act(0, ACT.Square, jj, jj + 1)
+            stt(0, jj, jj + 1)
+        for u in range(NU):
+            t, g = divmod(u, NG)
+            last = u == NU - 1
+            pe_b, v_b, s_b = blocks[u]
+            if u in (3, 5, 7):
+                mm0((u - 3) // 2, 0)
+                mm0((u - 3) // 2, 1)
+            if u in (4, 6):
+                mm0((u - 4) // 2, 2)
+                mm0((u - 4) // 2, 3)
+            if u == 3:
+                mm1(0, 0)
+            if u == 5:
+                mm1(1, 0)
+            if u == 6:
+                mm1(2, 0)
+            if u > 0:
+                stt(u)
+            tr(u, 0)
+            if pe_b:
+                il_pe(u, *pe_b[0])
+            if not last:
+                act(u + 1, ACT.Tanh, 0, 2)
+                act(u + 1, ACT.Tanh, 2, 4)
+                act(u + 1, ACT.Square, 0, 2)
+            if u == 0:
+                act(1, ACT.Square, 2, 4)
+                make_d2(1, "v")
+            cp(u, 0, "s")
+            tr(u, 1)
+            if not last and u > 0:
+                act(u + 1, ACT.Square, 2, 4)
+            if pe_b:
+                il_cp(u, *pe_b[0])
+            if len(pe_b) > 1:
+                il_pe(u, *pe_b[1])
+            cp(u, 1, "s")
+            if len(pe_b) > 1:
+                il_cp(u, *pe_b[1])
+            for r0, r1 in s_b:
+                il(u, r0, r1, "s")
+            if u == 0:
+                load_s(5)
+            if u >= 1:
+                q_r(u - 1)
+                q_t(u - 1)
+            for r0, r1 in v_b:
+                il(u, r0, r1, "v")
+            if u == 0:
+                q_d(0)
+            if u == 1:
+                q_d(1)
+                make_p(0, 0)
+                make_p(0, 1)
+            if u == 2:
+                q_p(0)
+                make_p(1, 0)
+            if u == 3:
+                make_p(1, 1)
+            if u == 4:
+                q_p(1)
+                make_p(2, 0)
+            if u == 5:
+                make_p(2, 1)
+                q_p(2)
+                make_p(3, 0)
+            if u == 6:
+                make_p(3, 1)
+                q_p(3)
+            if u in (3, 5, 7):
+                ev0((u - 3) // 2, 0)
+                ev0((u - 3) // 2, 1)
+            if u in (4, 6):
+                ev0((u - 4) // 2, 2)
+                ev0((u - 4) // 2, 3)
+                st0((u - 4) // 2, 0, 4)
+            if u == 1:
+                load_p(2)
+                load_s(6)
+                load_g(3)
+            if u == 2:
+                load_s(7)
+            if u == 3:
+                load_p(3)
+        mm1(3, 0)
+        mm0(2, 2)
+        mm0(2, 3)
+        for r in range(4):
+            ev1(0, r)
+        st1(0, 0, 4)
+        for tt in range(NT - 1):
+            mm1(tt, 1)
+        q_r(NU - 1)
+        q_t(NU - 1)
+        ev0(2, 2)
+        ev0(2, 3)
+        st0(2, 0, 4)
+        mm0(3, 0, spare=True)
+        mm0(3, 1, spare=True)
+        mm1(NT - 1, 1)
+        mm0(3, 2)
+        mm0(3, 3)
+        ev0(3, 0)
+        ev0(3, 1)
+        st0(3, 0, 2)
+        for r in range(4):
+            ev1(1, r)
+            if r % 2 == 1:
+                st1(1, r - 1, r + 1)
+        ev0(3, 2)
+        ev0(3, 3)
+        st0(3, 2, 4)

@@ -289,7 +289,7 @@ def tile_dedicomdecoder_v_kernel(tc, z_i, z_j, w_r, d_w, rz_in, scores, grad_out
 
         blocks = {0: ([], [(0, 4)], [])}
         for u in range(1, NU):
-            blocks[u] = ([(0, 2), (2, 3)], [(3, 4)], [])
+            blocks[u] = ([], [(2, 4)], [(0, 2)])
         make_d2(0)
         for jj in range(4):
             act(0, ACT.Tanh, jj, jj + 1)

@@ -37,66 +37,39 @@ def tile_dedicomdecoder_v_kernel(tc, z_i, z_j, w_r, d_w, rz_in, scores, grad_out
 
         s_t, g_t, z_t, rz_t = {}, {}, {}, {}
 
-        def load_s(u, pieces=1):
+        def load_s(u, j0=0, j1=4):
             t, g = divmod(u, NG)
-            tile = s_pool.tile([P, 4, 512], F32, name="s_tile")
+            if u not in s_t:
+                s_t[u] = s_pool.tile([P, 4, 512], F32, name="s_tile")
             src = scores[512 * t : 512 * (t + 1), 512 * g : 512 * (g + 1)].rearrange("(p j) n -> p j n", j=4)
-            w = 4 // pieces
-            for i in range(pieces):
-                nc.sync.dma_start(out=tile[:, w * i : w * (i + 1), :], in_=src[:, w * i : w * (i + 1), :])
-                if i == 0 and u == 0:
-                    load_d(0)
-            s_t[u] = tile
+            nc.sync.dma_start(out=s_t[u][:, j0:j1, :], in_=src[:, j0:j1, :])
 
         def load_d(g):
-            nc.sync.dma_start(
-                out=d_sb[:, g, :, :], in_=d_w[512 * g : 512 * (g + 1), :].rearrange("(p j) h -> p j h", j=4)
-            )
+            src = d_w[512 * g : 512 * (g + 1), :].rearrange("(p j) h -> p j h", j=4)
+            nc.sync.dma_start(out=d_sb[:, g, :, :], in_=src)
 
-        def load_g(t):
-            tile = three.tile([P, 4, R], BF16, name="g_tile")
+        def load_g(t, c0=0, c1=1024):
+            if t not in g_t:
+                g_t[t] = three.tile([P, 4, R], BF16, name="g_tile")
             src = grad_out[512 * t : 512 * (t + 1), :].rearrange("(p j) n -> p j n", j=4)
-            g_t[t] = tile
-            if t == 0:
-                nc.sync.dma_start(out=tile[:, :, 0:512], in_=src[:, :, 0:512])
-            else:
-                nc.sync.dma_start(out=tile[:], in_=src)
+            nc.sync.dma_start(out=g_t[t][:, :, c0:c1], in_=src[:, :, c0:c1])
 
-        def load_g0b():
-            src = grad_out[0:512, :].rearrange("(p j) n -> p j n", j=4)
-            nc.sync.dma_start(out=g_t[0][:, :, 512:1024], in_=src[:, :, 512:1024])
+        def load_z(t):
+            z_t[t] = two.tile([P, 4, H], BF16, name="z_tile")
+            nc.sync.dma_start(out=z_t[t][:], in_=z_i[512 * t : 512 * (t + 1), :].rearrange("(p j) n -> p j n", j=4))
 
-        def load_p(t):
-            tile = two.tile([P, 4, H], BF16, name="z_tile")
-            nc.sync.dma_start(out=tile[:], in_=z_i[512 * t : 512 * (t + 1), :].rearrange("(p j) n -> p j n", j=4))
-            z_t[t] = tile
-            tile2 = keep.tile([P, 4, H], F32, name="rz_tile%d" % t)
-            nc.sync.dma_start(out=tile2[:], in_=rz_in[512 * t : 512 * (t + 1), :].rearrange("(p j) n -> p j n", j=4))
-            rz_t[t] = tile2
+        def load_rz(t):
+            rz_t[t] = keep.tile([P, 4, H], F32, name="rz_tile%d" % t)
+            nc.sync.dma_start(out=rz_t[t][:], in_=rz_in[512 * t : 512 * (t + 1), :].rearrange("(p j) n -> p j n", j=4))
 
         ident = keep.tile([P, P], F32, name="ident")
         make_identity(nc, ident[:])
-        ident_b = keep.tile([P, P], BF16, name="ident_b")
-        make_identity(nc, ident_b[:])
         warm = keep.tile([P, 1], F32, name="warm")
         nc.vector.memset(warm[:], 0.0)
         warm2 = keep.tile([P, 1], F32, name="warm2")
         nc.scalar.activation(out=warm2[:], in_=warm[:], func=ACT.Tanh)
 
         d_sb = keep.tile([P, NG, 4, H], BF16, name="d_sb")
-        load_s(0, pieces=4)
-        load_g(0)
-        load_s(1)
-        load_d(1)
-        load_g0b()
-        load_s(2)
-        load_p(0)
-        load_g(1)
-        load_s(3)
-        load_s(4)
-        load_p(1)
-        load_g(2)
-
         d2_code = keep.tile([P, NG, H], U32, name="d2_code", align_bytes=64)
         d2_scale = keep.tile([P, NG, H], U8, name="d2_scale", align_bytes=64)
         p_code = keep.tile([P, NT, H], U32, name="p_code", align_bytes=64)
@@ -118,7 +91,7 @@ def tile_dedicomdecoder_v_kernel(tc, z_i, z_j, w_r, d_w, rz_in, scores, grad_out
 
         def stt(u, j0=0, j1=4):
             t, g = divmod(u, NG)
-            if j0 == 0:
+            if u not in dz_t:
                 dz_t[u] = three.tile([P, 4, 512], BF16, name="dz", align_bytes=64)
             j = slice(j0, j1)
             nc.vector.scalar_tensor_tensor(
@@ -129,20 +102,6 @@ def tile_dedicomdecoder_v_kernel(tc, z_i, z_j, w_r, d_w, rz_in, scores, grad_out
                 op0=ALU.subtract,
                 op1=ALU.mult,
             )
-
-        il_bank = {}
-
-        def il_pe(u, r0, r1):
-            if u not in dzi_t:
-                dzi_t[u] = two.tile([P, 4, P, 4], BF16, name="dzi", align_bytes=64)
-            src = dz_t[u][:].rearrange("p t (m r) -> p r m t", r=4)
-            bank = ps_wk.tile([P, r1 - r0, P, 4], BF16, name="bank")
-            for r in range(r0, r1):
-                nc.tensor.matmul(bank[:, r - r0, :, :], lhsT=ident_b[:], rhs=src[:, r, :, :], start=True, stop=True)
-            il_bank[u, r0] = bank
-
-        def il_cp(u, r0, r1):
-            nc.scalar.copy(out=dzi_t[u][:, r0:r1, :, :], in_=il_bank[u, r0][:])
 
         def il(u, r0, r1, eng):
             if r0 == r1:
@@ -171,7 +130,7 @@ def tile_dedicomdecoder_v_kernel(tc, z_i, z_j, w_r, d_w, rz_in, scores, grad_out
                 for h in range(2):
                     nc.tensor.transpose(bank[:, jj, h, :], words[:, w0 + h : w0 + 256 : 2], ident[:])
             tr_t[u, b] = bank
-            if b == 0:
+            if u not in dzr_t:
                 dzr_t[u] = two.tile([P, 4, P, 4], BF16, name="dzr", align_bytes=64)
 
         def cp(u, b, eng):
@@ -191,7 +150,7 @@ def tile_dedicomdecoder_v_kernel(tc, z_i, z_j, w_r, d_w, rz_in, scores, grad_out
             )
 
         def make_p(t, half):
-            if half == 0:
+            if t not in p_t:
                 p_t[t] = two.tile([P, H, 4], BF16, name="p_tile", align_bytes=64)
             cols = slice(256 * half, 256 * (half + 1))
             nc.vector.tensor_tensor(
@@ -246,9 +205,17 @@ def tile_dedicomdecoder_v_kernel(tc, z_i, z_j, w_r, d_w, rz_in, scores, grad_out
                 )
             o0_bank[t, j] = bank
 
-        def ev0(t, j):
-            if j == 0:
+        def ev_help(bank, factor, other, dst):
+            tmp = two.tile([P, H], F32, name="ev_tmp")
+            nc.scalar.activation(out=tmp[:], in_=bank, func=ACT.Copy, scale=factor)
+            nc.gpsimd.tensor_tensor(out=dst, in0=tmp[:], in1=other, op=ALU.mult)
+
+        def ev0(t, j, helped=False):
+            if t not in o0_t:
                 o0_t[t] = two.tile([P, 4, H], F32, name="o0_tile")
+            if helped:
+                ev_help(o0_bank[t, j][:], -1.0, rz_t[t][:, j, :], o0_t[t][:, j, :])
+                return
             nc.vector.scalar_tensor_tensor(
                 out=o0_t[t][:, j, :], in0=o0_bank[t, j][:], scalar=-1.0, in1=rz_t[t][:, j, :], op0=ALU.mult, op1=ALU.mult
             )
@@ -276,9 +243,12 @@ def tile_dedicomdecoder_v_kernel(tc, z_i, z_j, w_r, d_w, rz_in, scores, grad_out
 
         o1_t = {}
 
-        def ev1(g, r):
-            if r == 0:
+        def ev1(g, r, helped=False):
+            if g not in o1_t:
                 o1_t[g] = two.tile([P, 4, H], F32, name="o1_tile")
+            if helped:
+                ev_help(acc[g, r][:], -2.0, d_sb[:, g, r, :], o1_t[g][:, r, :])
+                return
             nc.vector.scalar_tensor_tensor(
                 out=o1_t[g][:, r, :], in0=acc[g, r][:], scalar=-2.0, in1=d_sb[:, g, r, :], op0=ALU.mult, op1=ALU.mult
             )
@@ -287,123 +257,211 @@ def tile_dedicomdecoder_v_kernel(tc, z_i, z_j, w_r, d_w, rz_in, scores, grad_out
             dst = out_1[512 * g : 512 * (g + 1), :].rearrange("(m r) h -> m r h", r=4)
             nc.sync.dma_start(out=dst[:, r0:r1, :], in_=o1_t[g][:, r0:r1, :])
 
-        blocks = {0: ([], [(0, 4)], [])}
-        for u in range(1, NU):
-            blocks[u] = ([], [(2, 4)], [(0, 2)])
+        load_s(0, 0, 1)
+        act(0, ACT.Tanh, 0, 1)
+        act(0, ACT.Square, 0, 1)
+        load_d(0)
         make_d2(0)
-        for jj in range(4):
-            act(0, ACT.Tanh, jj, jj + 1)
-            act(0, ACT.Square, jj, jj + 1)
-            stt(0, jj, jj + 1)
-        for u in range(NU):
-            t, g = divmod(u, NG)
-            last = u == NU - 1
-            pe_b, v_b, s_b = blocks[u]
-            if u in (3, 5, 7):
-                mm0((u - 3) // 2, 0)
-                mm0((u - 3) // 2, 1)
-            if u in (4, 6):
-                mm0((u - 4) // 2, 2)
-                mm0((u - 4) // 2, 3)
-            if u == 3:
-                mm1(0, 0)
-            if u == 5:
-                mm1(1, 0)
-            if u == 6:
-                mm1(2, 0)
-            if u > 0:
-                stt(u)
-            tr(u, 0)
-            if pe_b:
-                il_pe(u, *pe_b[0])
-            if not last:
-                act(u + 1, ACT.Tanh, 0, 2)
-                act(u + 1, ACT.Tanh, 2, 4)
-                act(u + 1, ACT.Square, 0, 2)
-            if u == 0:
-                act(1, ACT.Square, 2, 4)
-                make_d2(1, "v")
-            cp(u, 0, "s")
-            tr(u, 1)
-            if not last and u > 0:
-                act(u + 1, ACT.Square, 2, 4)
-            if pe_b:
-                il_cp(u, *pe_b[0])
-            if len(pe_b) > 1:
-                il_pe(u, *pe_b[1])
-            cp(u, 1, "s")
-            if len(pe_b) > 1:
-                il_cp(u, *pe_b[1])
-            for r0, r1 in s_b:
-                il(u, r0, r1, "s")
-            if u == 0:
-                load_s(5)
-            if u >= 1:
-                q_r(u - 1)
-                q_t(u - 1)
-            for r0, r1 in v_b:
-                il(u, r0, r1, "v")
-            if u == 0:
-                q_d(0)
-            if u == 1:
-                q_d(1)
-                make_p(0, 0)
-                make_p(0, 1)
-            if u == 2:
-                q_p(0)
-                make_p(1, 0)
-            if u == 3:
-                make_p(1, 1)
-            if u == 4:
-                q_p(1)
-                make_p(2, 0)
-            if u == 5:
-                make_p(2, 1)
-                q_p(2)
-                make_p(3, 0)
-            if u == 6:
-                make_p(3, 1)
-                q_p(3)
-            if u in (3, 5, 7):
-                ev0((u - 3) // 2, 0)
-                ev0((u - 3) // 2, 1)
-            if u in (4, 6):
-                ev0((u - 4) // 2, 2)
-                ev0((u - 4) // 2, 3)
-                st0((u - 4) // 2, 0, 4)
-            if u == 1:
-                load_p(2)
-                load_s(6)
-                load_g(3)
-            if u == 2:
-                load_s(7)
-            if u == 3:
-                load_p(3)
+        q_d(0)
+        load_s(0, 3, 4)
+        act(0, ACT.Tanh, 3, 4)
+        act(0, ACT.Square, 3, 4)
+        load_s(0, 1, 2)
+        act(0, ACT.Tanh, 1, 2)
+        act(0, ACT.Square, 1, 2)
+        load_g(0, 0, 512)
+        load_s(0, 2, 3)
+        act(0, ACT.Tanh, 2, 3)
+        act(0, ACT.Square, 2, 3)
+        stt(0, 0, 1)
+        stt(0, 1, 2)
+        tr(0, 0)
+        cp(0, 0, "s")
+        load_s(1)
+        act(1, ACT.Tanh, 0, 2)
+        load_d(1)
+        load_g(0, 512, 1024)
+        load_s(2)
+        load_z(0)
+        load_rz(0)
+        stt(0, 3, 4)
+        stt(0, 2, 3)
+        tr(0, 1)
+        il(0, 0, 4, "v")
+        make_d2(1)
+        q_t(0)
+        q_d(1)
+        act(1, ACT.Tanh, 2, 4)
+        act(1, ACT.Square, 0, 2)
+        act(1, ACT.Square, 2, 4)
+        stt(1)
+        il(1, 1, 4, "v")
+        cp(0, 1, "s")
+        q_r(0)
+        make_p(0, 0)
+        act(2, ACT.Tanh, 0, 2)
+        act(2, ACT.Tanh, 2, 4)
+        act(2, ACT.Square, 0, 2)
+        tr(1, 0)
+        tr(1, 1)
+        cp(1, 0, "s")
+        cp(1, 1, "s")
+        q_r(1)
+        mm0(0, 0)
+        mm0(0, 1)
+        make_p(0, 1)
+        ev0(0, 0)
+        act(2, ACT.Square, 2, 4)
+        il(1, 0, 1, "s")
+        q_t(1)
+        q_p(0)
+        mm1(0, 0)
+        load_s(3)
+        act(3, ACT.Tanh, 0, 2)
+        act(3, ACT.Tanh, 2, 4)
+        ev0(0, 1)
+        mm0(0, 2)
+        mm0(0, 3)
+        act(3, ACT.Square, 0, 2)
+        act(3, ACT.Square, 2, 4)
+        load_g(1)
+        stt(2)
+        tr(2, 0)
+        stt(3)
+        load_s(4)
+        act(4, ACT.Tanh, 0, 2)
+        act(4, ACT.Tanh, 2, 4)
+        load_z(1)
+        load_rz(1)
+        ev0(0, 2)
+        make_p(1, 0)
+        il(3, 2, 4, "v")
+        il(2, 1, 4, "v")
+        make_p(1, 1)
+        ev0(0, 3)
+        cp(2, 0, "s")
+        tr(2, 1)
+        tr(3, 0)
+        cp(2, 1, "s")
+        tr(3, 1)
+        q_r(2)
+        il(2, 0, 1, "s")
+        il(3, 0, 2, "s")
+        q_p(1)
+        q_t(2)
+        load_s(5)
+        load_g(2)
+        act(4, ACT.Square, 2, 4)
+        act(4, ACT.Square, 0, 2)
+        act(5, ACT.Tanh, 2, 4)
+        stt(4)
+        load_rz(2)
+        load_z(2)
+        make_p(2, 1)
+        q_t(3)
+        mm1(1, 0)
+        act(5, ACT.Tanh, 0, 2)
+        cp(3, 1, "s")
+        cp(3, 0, "s")
+        tr(4, 0)
+        q_r(3)
+        tr(4, 1)
+        mm0(1, 0)
+        mm0(1, 1)
+        act(5, ACT.Square, 2, 4)
+        act(5, ACT.Square, 0, 2)
+        stt(5)
+        make_p(2, 0)
+        cp(4, 0, "s")
+        il(4, 0, 2, "s")
+        load_s(6)
+        act(6, ACT.Tanh, 2, 4)
+        load_s(7)
+        act(6, ACT.Tanh, 0, 2)
+        act(7, ACT.Tanh, 2, 4)
+        ev0(1, 0)
+        mm0(1, 2)
+        ev0(1, 1)
+        il(4, 2, 4, "v")
+        ev0(1, 2)
+        load_z(3)
+        load_rz(3)
+        make_p(3, 0)
+        make_p(3, 1)
+        act(6, ACT.Square, 0, 2)
+        act(6, ACT.Square, 2, 4)
+        cp(4, 1, "s")
+        tr(5, 0)
+        mm0(1, 3)
+        tr(5, 1)
+        q_p(2)
+        q_t(4)
+        mm1(2, 0)
+        ev0(1, 3)
+        q_p(3)
+        il(5, 3, 4, "v")
+        cp(5, 0, "s")
+        act(7, ACT.Tanh, 0, 2)
+        il(5, 0, 3, "s")
+        cp(5, 1, "s")
+        act(7, ACT.Square, 2, 4)
+        act(7, ACT.Square, 0, 2)
+        load_g(3)
+        stt(6)
+        il(6, 0, 4, "s")
+        tr(6, 0)
+        q_r(4)
+        cp(6, 0, "s")
+        q_t(5)
+        q_r(5)
+        mm0(2, 0)
+        mm0(2, 1)
+        stt(7)
+        il(7, 0, 2, "s")
+        tr(6, 1)
+        tr(7, 0)
+        q_t(6)
         mm1(3, 0)
+        st0(0, 0, 4)
+        ev0(2, 1)
+        st0(1, 0, 4)
+        ev0(2, 0)
         mm0(2, 2)
+        cp(6, 1, "s")
+        tr(7, 1)
         mm0(2, 3)
-        for r in range(4):
-            ev1(0, r)
+        ev1(0, 1)
+        ev1(0, 0)
+        ev1(0, 3)
+        ev1(0, 2)
         st1(0, 0, 4)
-        for tt in range(NT - 1):
-            mm1(tt, 1)
-        q_r(NU - 1)
-        q_t(NU - 1)
-        ev0(2, 2)
+        mm1(0, 1)
+        mm1(1, 1)
+        q_r(6)
         ev0(2, 3)
-        st0(2, 0, 4)
+        cp(7, 0, "s")
+        cp(7, 1, "s")
+        q_r(7)
         mm0(3, 0, spare=True)
         mm0(3, 1, spare=True)
-        mm1(NT - 1, 1)
-        mm0(3, 2)
-        mm0(3, 3)
+        ev0(2, 2)
+        st0(2, 0, 4)
+        il(7, 2, 4, "v")
         ev0(3, 0)
+        q_t(7)
         ev0(3, 1)
         st0(3, 0, 2)
-        for r in range(4):
-            ev1(1, r)
-            if r % 2 == 1:
-                st1(1, r - 1, r + 1)
+        mm1(2, 1)
+        mm1(3, 1)
+        ev1(1, 0)
+        ev1(1, 1)
+        st1(1, 0, 2)
+        ev1(1, 2)
+        ev1(1, 3)
+        st1(1, 2, 4)
+        mm0(3, 2)
+        mm0(3, 3)
         ev0(3, 2)
+        st0(3, 2, 3)
         ev0(3, 3)
-        st0(3, 2, 4)
+        st0(3, 3, 4)

@@ -205,17 +205,9 @@ def tile_dedicomdecoder_v_kernel(tc, z_i, z_j, w_r, d_w, rz_in, scores, grad_out
                 )
             o0_bank[t, j] = bank
 
-        def ev_help(bank, factor, other, dst):
-            tmp = two.tile([P, H], F32, name="ev_tmp")
-            nc.scalar.activation(out=tmp[:], in_=bank, func=ACT.Copy, scale=factor)
-            nc.gpsimd.tensor_tensor(out=dst, in0=tmp[:], in1=other, op=ALU.mult)
-
-        def ev0(t, j, helped=False):
+        def ev0(t, j):
             if t not in o0_t:
                 o0_t[t] = two.tile([P, 4, H], F32, name="o0_tile")
-            if helped:
-                ev_help(o0_bank[t, j][:], -1.0, rz_t[t][:, j, :], o0_t[t][:, j, :])
-                return
             nc.vector.scalar_tensor_tensor(
                 out=o0_t[t][:, j, :], in0=o0_bank[t, j][:], scalar=-1.0, in1=rz_t[t][:, j, :], op0=ALU.mult, op1=ALU.mult
             )
@@ -243,12 +235,9 @@ def tile_dedicomdecoder_v_kernel(tc, z_i, z_j, w_r, d_w, rz_in, scores, grad_out
 
         o1_t = {}
 
-        def ev1(g, r, helped=False):
+        def ev1(g, r):
             if g not in o1_t:
                 o1_t[g] = two.tile([P, 4, H], F32, name="o1_tile")
-            if helped:
-                ev_help(acc[g, r][:], -2.0, d_sb[:, g, r, :], o1_t[g][:, r, :])
-                return
             nc.vector.scalar_tensor_tensor(
                 out=o1_t[g][:, r, :], in0=acc[g, r][:], scalar=-2.0, in1=d_sb[:, g, r, :], op0=ALU.mult, op1=ALU.mult
             )
@@ -262,206 +251,206 @@ def tile_dedicomdecoder_v_kernel(tc, z_i, z_j, w_r, d_w, rz_in, scores, grad_out
         act(0, ACT.Square, 0, 1)
         load_d(0)
         make_d2(0)
-        q_d(0)
         load_s(0, 3, 4)
         act(0, ACT.Tanh, 3, 4)
-        act(0, ACT.Square, 3, 4)
         load_s(0, 1, 2)
         act(0, ACT.Tanh, 1, 2)
         act(0, ACT.Square, 1, 2)
+        act(0, ACT.Square, 3, 4)
         load_g(0, 0, 512)
+        stt(0, 0, 1)
         load_s(0, 2, 3)
         act(0, ACT.Tanh, 2, 3)
         act(0, ACT.Square, 2, 3)
-        stt(0, 0, 1)
         stt(0, 1, 2)
         tr(0, 0)
         cp(0, 0, "s")
         load_s(1)
-        act(1, ACT.Tanh, 0, 2)
-        load_d(1)
-        load_g(0, 512, 1024)
-        load_s(2)
-        load_z(0)
-        load_rz(0)
+        act(1, ACT.Tanh, 2, 4)
+        q_d(0)
         stt(0, 3, 4)
         stt(0, 2, 3)
         tr(0, 1)
         il(0, 0, 4, "v")
+        load_d(1)
         make_d2(1)
         q_t(0)
         q_d(1)
-        act(1, ACT.Tanh, 2, 4)
-        act(1, ACT.Square, 0, 2)
+        act(1, ACT.Tanh, 0, 2)
         act(1, ACT.Square, 2, 4)
+        load_g(0, 512, 1024)
+        act(1, ACT.Square, 0, 2)
         stt(1)
-        il(1, 1, 4, "v")
+        tr(1, 0)
         cp(0, 1, "s")
+        tr(1, 1)
         q_r(0)
-        make_p(0, 0)
+        load_s(2)
         act(2, ACT.Tanh, 0, 2)
         act(2, ACT.Tanh, 2, 4)
         act(2, ACT.Square, 0, 2)
-        tr(1, 0)
-        tr(1, 1)
-        cp(1, 0, "s")
+        il(1, 1, 4, "v")
+        load_z(0)
+        load_rz(0)
+        make_p(0, 0)
+        make_p(0, 1)
+        act(2, ACT.Square, 2, 4)
         cp(1, 1, "s")
+        cp(1, 0, "s")
         q_r(1)
         mm0(0, 0)
         mm0(0, 1)
-        make_p(0, 1)
-        ev0(0, 0)
-        act(2, ACT.Square, 2, 4)
+        q_p(0)
         il(1, 0, 1, "s")
         q_t(1)
-        q_p(0)
-        mm1(0, 0)
+        ev0(0, 0)
+        mm0(0, 2)
         load_s(3)
         act(3, ACT.Tanh, 0, 2)
         act(3, ACT.Tanh, 2, 4)
-        ev0(0, 1)
-        mm0(0, 2)
-        mm0(0, 3)
         act(3, ACT.Square, 0, 2)
-        act(3, ACT.Square, 2, 4)
         load_g(1)
         stt(2)
         tr(2, 0)
-        stt(3)
+        tr(2, 1)
+        ev0(0, 1)
+        act(3, ACT.Square, 2, 4)
         load_s(4)
         act(4, ACT.Tanh, 0, 2)
         act(4, ACT.Tanh, 2, 4)
-        load_z(1)
-        load_rz(1)
-        ev0(0, 2)
-        make_p(1, 0)
-        il(3, 2, 4, "v")
-        il(2, 1, 4, "v")
-        make_p(1, 1)
-        ev0(0, 3)
         cp(2, 0, "s")
-        tr(2, 1)
-        tr(3, 0)
-        cp(2, 1, "s")
-        tr(3, 1)
-        q_r(2)
-        il(2, 0, 1, "s")
+        stt(3)
         il(3, 0, 2, "s")
-        q_p(1)
-        q_t(2)
-        load_s(5)
+        act(4, ACT.Square, 0, 2)
+        ev0(0, 2)
+        il(3, 2, 4, "v")
+        cp(2, 1, "s")
+        mm0(0, 3)
+        ev0(0, 3)
+        il(2, 1, 4, "v")
+        load_rz(1)
+        load_z(1)
+        make_p(1, 0)
+        q_r(2)
+        make_p(1, 1)
+        tr(3, 0)
+        il(2, 0, 1, "s")
         load_g(2)
         act(4, ACT.Square, 2, 4)
-        act(4, ACT.Square, 0, 2)
-        act(5, ACT.Tanh, 2, 4)
         stt(4)
-        load_rz(2)
-        load_z(2)
-        make_p(2, 1)
-        q_t(3)
-        mm1(1, 0)
-        act(5, ACT.Tanh, 0, 2)
+        q_p(1)
+        tr(3, 1)
         cp(3, 1, "s")
         cp(3, 0, "s")
-        tr(4, 0)
         q_r(3)
+        tr(4, 0)
         tr(4, 1)
-        mm0(1, 0)
-        mm0(1, 1)
+        load_s(5)
+        act(5, ACT.Tanh, 2, 4)
         act(5, ACT.Square, 2, 4)
+        act(5, ACT.Tanh, 0, 2)
         act(5, ACT.Square, 0, 2)
-        stt(5)
-        make_p(2, 0)
         cp(4, 0, "s")
+        q_t(3)
         il(4, 0, 2, "s")
+        q_t(2)
+        cp(4, 1, "s")
+        load_rz(2)
+        load_z(2)
+        make_p(2, 0)
         load_s(6)
-        act(6, ACT.Tanh, 2, 4)
-        load_s(7)
         act(6, ACT.Tanh, 0, 2)
-        act(7, ACT.Tanh, 2, 4)
+        load_s(7)
+        act(7, ACT.Tanh, 0, 2)
+        mm0(1, 0)
         ev0(1, 0)
+        mm0(1, 1)
         mm0(1, 2)
+        make_p(2, 1)
         ev0(1, 1)
+        stt(5)
         il(4, 2, 4, "v")
+        mm0(1, 3)
+        q_r(4)
         ev0(1, 2)
+        q_p(2)
+        mm1(0, 0)
+        tr(5, 0)
+        mm1(1, 0)
+        tr(5, 1)
+        q_t(4)
+        mm1(2, 0)
         load_z(3)
         load_rz(3)
         make_p(3, 0)
         make_p(3, 1)
+        act(6, ACT.Tanh, 2, 4)
         act(6, ACT.Square, 0, 2)
-        act(6, ACT.Square, 2, 4)
-        cp(4, 1, "s")
-        tr(5, 0)
-        mm0(1, 3)
-        tr(5, 1)
-        q_p(2)
-        q_t(4)
-        mm1(2, 0)
-        ev0(1, 3)
-        q_p(3)
-        il(5, 3, 4, "v")
-        cp(5, 0, "s")
-        act(7, ACT.Tanh, 0, 2)
-        il(5, 0, 3, "s")
-        cp(5, 1, "s")
-        act(7, ACT.Square, 2, 4)
-        act(7, ACT.Square, 0, 2)
+        act(7, ACT.Tanh, 2, 4)
         load_g(3)
+        act(6, ACT.Square, 2, 4)
         stt(6)
-        il(6, 0, 4, "s")
+        cp(5, 0, "s")
         tr(6, 0)
-        q_r(4)
-        cp(6, 0, "s")
-        q_t(5)
+        cp(5, 1, "s")
+        tr(6, 1)
+        ev0(1, 3)
         q_r(5)
         mm0(2, 0)
         mm0(2, 1)
+        act(7, ACT.Square, 2, 4)
+        il(5, 3, 4, "v")
+        act(7, ACT.Square, 0, 2)
         stt(7)
-        il(7, 0, 2, "s")
-        tr(6, 1)
-        tr(7, 0)
+        il(6, 0, 4, "s")
         q_t(6)
+        cp(6, 0, "s")
+        tr(7, 0)
+        cp(6, 1, "s")
+        tr(7, 1)
+        cp(7, 1, "s")
+        q_p(3)
         mm1(3, 0)
         st0(0, 0, 4)
         ev0(2, 1)
-        st0(1, 0, 4)
         ev0(2, 0)
         mm0(2, 2)
-        cp(6, 1, "s")
-        tr(7, 1)
         mm0(2, 3)
-        ev1(0, 1)
+        q_r(6)
         ev1(0, 0)
-        ev1(0, 3)
+        ev1(0, 1)
         ev1(0, 2)
+        st0(1, 0, 4)
+        ev1(0, 3)
         st1(0, 0, 4)
         mm1(0, 1)
-        mm1(1, 1)
-        q_r(6)
-        ev0(2, 3)
         cp(7, 0, "s")
-        cp(7, 1, "s")
         q_r(7)
-        mm0(3, 0, spare=True)
-        mm0(3, 1, spare=True)
+        il(5, 0, 3, "s")
+        q_t(5)
         ev0(2, 2)
+        ev0(2, 3)
         st0(2, 0, 4)
         il(7, 2, 4, "v")
-        ev0(3, 0)
-        q_t(7)
+        il(7, 0, 2, "s")
+        mm0(3, 0, spare=True)
+        mm0(3, 1, spare=True)
         ev0(3, 1)
+        q_t(7)
+        ev0(3, 0)
         st0(3, 0, 2)
+        mm1(1, 1)
         mm1(2, 1)
         mm1(3, 1)
         ev1(1, 0)
         ev1(1, 1)
         st1(1, 0, 2)
-        ev1(1, 2)
         ev1(1, 3)
+        ev1(1, 2)
         st1(1, 2, 4)
         mm0(3, 2)
-        mm0(3, 3)
         ev0(3, 2)
         st0(3, 2, 3)
+        mm0(3, 3)
         ev0(3, 3)
         st0(3, 3, 4)

from contextlib import ExitStack

import concourse.mybir as mybir
from concourse.masks import make_identity

B, H, R = 2048, 512, 1024

FLOPS = 2 * 2 * B * H * R
BYTES = 2 * B * H + 2 * R * H + 4 * B * H + 4 * B * R + 2 * B * R + 4 * B * H + 4 * R * H

F32 = mybir.dt.float32
BF16 = mybir.dt.bfloat16
U32 = mybir.dt.uint32
U8 = mybir.dt.uint8
E4M3 = mybir.dt.float8_e4m3fn_x4
E5M2 = mybir.dt.float8_e5m2_x4
ACT = mybir.ActivationFunctionType
ALU = mybir.AluOpType

P = 128
NT = B // 512
NG = R // 512
NU = NT * NG


def tile_dedicomdecoder_v_kernel(tc, z_i, z_j, w_r, d_w, rz_in, scores, grad_out, out_0, out_1):
    nc = tc.nc
    with ExitStack() as ctx:
        keep = ctx.enter_context(tc.tile_pool(name="keep", bufs=1))
        s_pool = ctx.enter_context(tc.tile_pool(name="s_pool", bufs=5))
        three = ctx.enter_context(tc.tile_pool(name="three", bufs=3))
        two = ctx.enter_context(tc.tile_pool(name="two", bufs=2))
        ps_wk = ctx.enter_context(tc.psum_pool(name="ps_wk", bufs=2))
        ps_o0 = ctx.enter_context(tc.psum_pool(name="ps_o0", bufs=2))
        ps_acc = ctx.enter_context(tc.psum_pool(name="ps_acc", bufs=1))
        ctx.enter_context(tc.manual_schedule())

        s_t, g_t, z_t, rz_t = {}, {}, {}, {}

        def load_s(u, j0=0, j1=4):
            t, g = divmod(u, NG)
            if u not in s_t:
                s_t[u] = s_pool.tile([P, 4, 512], F32, name="s_tile")
            src = scores[512 * t : 512 * (t + 1), 512 * g : 512 * (g + 1)].rearrange("(p j) n -> p j n", j=4)
            nc.sync.dma_start(out=s_t[u][:, j0:j1, :], in_=src[:, j0:j1, :])

        def load_d(g):
            src = d_w[512 * g : 512 * (g + 1), :].rearrange("(p j) h -> p j h", j=4)
            nc.sync.dma_start(out=d_sb[:, g, :, :], in_=src)

        def load_g(t, c0=0, c1=1024):
            if t not in g_t:
                g_t[t] = three.tile([P, 4, R], BF16, name="g_tile")
            src = grad_out[512 * t : 512 * (t + 1), :].rearrange("(p j) n -> p j n", j=4)
            nc.sync.dma_start(out=g_t[t][:, :, c0:c1], in_=src[:, :, c0:c1])

        def load_z(t):
            z_t[t] = two.tile([P, 4, H], BF16, name="z_tile")
            nc.sync.dma_start(out=z_t[t][:], in_=z_i[512 * t : 512 * (t + 1), :].rearrange("(p j) n -> p j n", j=4))

        def load_rz(t):
            rz_t[t] = keep.tile([P, 4, H], F32, name="rz_tile%d" % t)
            nc.sync.dma_start(out=rz_t[t][:], in_=rz_in[512 * t : 512 * (t + 1), :].rearrange("(p j) n -> p j n", j=4))

        ident = keep.tile([P, P], F32, name="ident")
        make_identity(nc, ident[:])
        warm = keep.tile([P, 1], F32, name="warm")
        nc.vector.memset(warm[:], 0.0)
        warm2 = keep.tile([P, 1], F32, name="warm2")
        nc.scalar.activation(out=warm2[:], in_=warm[:], func=ACT.Tanh)

        d_sb = keep.tile([P, NG, 4, H], BF16, name="d_sb")
        d2_code = keep.tile([P, NG, H], U32, name="d2_code", align_bytes=64)
        d2_scale = keep.tile([P, NG, H], U8, name="d2_scale", align_bytes=64)
        p_code = keep.tile([P, NT, H], U32, name="p_code", align_bytes=64)
        p_scale = keep.tile([P, NT, H], U8, name="p_scale", align_bytes=64)
        t_code = keep.tile([P, NT + 2, 512], U32, name="t_code", align_bytes=64)
        t_scale = keep.tile([P, NT + 2, 512], U8, name="t_scale", align_bytes=64)
        r_code = keep.tile([P, 4, 512], U32, name="r_code", align_bytes=64)
        r_scale = keep.tile([P, 4, 512], U8, name="r_scale", align_bytes=64)

        def act(u, func, j0, j1):
            s = s_t[u][:, j0:j1, :]
            nc.scalar.activation(out=s, in_=s, func=func, scale=0.5)

        dz_t, dzi_t, dzr_t, p_t, tr_t = {}, {}, {}, {}, {}

        def slot(u):
            t, g = divmod(u, NG)
            return t if g == 1 else NT + t % 2

        def stt(u, j0=0, j1=4):
            t, g = divmod(u, NG)
            if u not in dz_t:
                dz_t[u] = three.tile([P, 4, 512], BF16, name="dz", align_bytes=64)
            j = slice(j0, j1)
            nc.vector.scalar_tensor_tensor(
                out=dz_t[u][:, j, :],
                in0=s_t[u][:, j, :],
                scalar=0.25,
                in1=g_t[t][:, j, 512 * g : 512 * (g + 1)],
                op0=ALU.subtract,
                op1=ALU.mult,
            )

        def il(u, r0, r1, eng):
            if r0 == r1:
                return
            if u not in dzi_t:
                dzi_t[u] = two.tile([P, 4, P, 4], BF16, name="dzi", align_bytes=64)
            dst = dzi_t[u][:, r0:r1, :, :].rearrange("p r m t -> p m t r")
            src = dz_t[u][:].rearrange("p t (m r) -> p m t r", r=4)[:, :, :, r0:r1]
            if eng == "s":
                nc.scalar.copy(out=dst, in_=src)
            else:
                nc.vector.tensor_copy(out=dst, in_=src)

        def q_t(u):
            nc.vector.quantize_mx(
                out=t_code[:, slot(u), :].bitcast(E5M2),
                scales=t_scale[:, slot(u), :],
                in_=dzi_t[u][:].rearrange("p r m t -> p (r m t)"),
            )

        def tr(u, b):
            words = dz_t[u][:].rearrange("p j n -> p (j n)").bitcast(F32)
            bank = ps_wk.tile([P, 2, 2, P], F32, name="bank")
            for jj in range(2):
                w0 = 256 * (2 * b + jj)
                for h in range(2):
                    nc.tensor.transpose(bank[:, jj, h, :], words[:, w0 + h : w0 + 256 : 2], ident[:])
            tr_t[u, b] = bank
            if u not in dzr_t:
                dzr_t[u] = two.tile([P, 4, P, 4], BF16, name="dzr", align_bytes=64)

        def cp(u, b, eng):
            src = tr_t[u, b][:].rearrange("m j h p -> m j p h")
            dst = dzr_t[u][:].rearrange("m j p r -> m (j p r)").bitcast(F32)[:, 512 * b : 512 * (b + 1)]
            dst = dst.rearrange("m (j p h) -> m j p h", j=2, h=2)
            if eng == "s":
                nc.scalar.copy(out=dst, in_=src)
            else:
                nc.vector.tensor_copy(out=dst, in_=src)

        def q_r(u, j0=0, j1=4):
            nc.vector.quantize_mx(
                out=r_code[:, u % 4, P * j0 : P * j1].bitcast(E5M2),
                scales=r_scale[:, u % 4, P * j0 : P * j1],
                in_=dzr_t[u][:, j0:j1, :, :].rearrange("m j p r -> m (j p r)"),
            )

        def make_p(t, half):
            if t not in p_t:
                p_t[t] = two.tile([P, H, 4], BF16, name="p_tile", align_bytes=64)
            cols = slice(256 * half, 256 * (half + 1))
            nc.vector.tensor_tensor(
                out=p_t[t][:, cols, :].rearrange("p (c i) t -> p c t i", i=4),
                in0=z_t[t][:, :, cols].rearrange("p t (c i) -> p c t i", i=4),
                in1=rz_t[t][:, :, cols].rearrange("p t (c i) -> p c t i", i=4),
                op=ALU.mult,
            )

        def q_p(t):
            nc.vector.quantize_mx(
                out=p_code[:, t, :].bitcast(E4M3),
                scales=p_scale[:, t, :],
                in_=p_t[t][:].rearrange("p h t -> p (h t)"),
            )

        d2_t = {}

        def make_d2(g, eng="v"):
            d2 = two.tile([P, H, 4], BF16, name="d2", align_bytes=64)
            v = d_sb[:, g, :, :].rearrange("p t (c i) -> p c t i", i=4)
            if eng == "s":
                nc.scalar.activation(out=d2[:].rearrange("p (c i) t -> p c t i", i=4), in_=v, func=ACT.Square)
            else:
                nc.vector.tensor_tensor(out=d2[:].rearrange("p (c i) t -> p c t i", i=4), in0=v, in1=v, op=ALU.mult)
            d2_t[g] = d2

        def q_d(g):
            nc.vector.quantize_mx(
                out=d2_code[:, g, :].bitcast(E4M3),
                scales=d2_scale[:, g, :],
                in_=d2_t[g][:].rearrange("p h t -> p (h t)"),
            )

        o0_t, o0_bank = {}, {}

        def mm0(t, j, spare=False):
            if spare:
                bank = ps_wk.tile([P, H], F32, name="bank")
            else:
                bank = ps_o0.tile([P, H], F32, name="o0_bank_tile")
            for g in range(NG):
                u = NG * t + g
                nc.tensor.matmul_mx(
                    out=bank[:],
                    lhsT=r_code[:, u % 4, P * j : P * (j + 1)].bitcast(E5M2),
                    lhsT_scale=r_scale[:, u % 4, P * j : P * (j + 1)],
                    rhs=d2_code[:, g, :].bitcast(E4M3),
                    rhs_scale=d2_scale[:, g, :],
                    start=(g == 0),
                    stop=(g == NG - 1),
                )
            o0_bank[t, j] = bank

        def ev0(t, j):
            if t not in o0_t:
                o0_t[t] = two.tile([P, 4, H], F32, name="o0_tile")
            nc.vector.scalar_tensor_tensor(
                out=o0_t[t][:, j, :], in0=o0_bank[t, j][:], scalar=-1.0, in1=rz_t[t][:, j, :], op0=ALU.mult, op1=ALU.mult
            )

        def st0(t, j0, j1):
            dst = out_0[512 * t : 512 * (t + 1), :].rearrange("(p j) h -> p j h", j=4)
            nc.sync.dma_start(out=dst[:, j0:j1, :], in_=o0_t[t][:, j0:j1, :])

        acc = {}

        def mm1(t, g):
            u = NG * t + g
            for r in range(4):
                if t == 0:
                    acc[g, r] = ps_acc.tile([P, H], F32, name="acc%d" % r)
                nc.tensor.matmul_mx(
                    out=acc[g, r][:],
                    lhsT=t_code[:, slot(u), P * r : P * (r + 1)].bitcast(E5M2),
                    lhsT_scale=t_scale[:, slot(u), P * r : P * (r + 1)],
                    rhs=p_code[:, t, :].bitcast(E4M3),
                    rhs_scale=p_scale[:, t, :],
                    start=(t == 0),
                    stop=(t == NT - 1),
                )

        o1_t = {}

        def ev1(g, r):
            if g not in o1_t:
                o1_t[g] = two.tile([P, 4, H], F32, name="o1_tile")
            nc.vector.scalar_tensor_tensor(
                out=o1_t[g][:, r, :], in0=acc[g, r][:], scalar=-2.0, in1=d_sb[:, g, r, :], op0=ALU.mult, op1=ALU.mult
            )

        def st1(g, r0, r1):
            dst = out_1[512 * g : 512 * (g + 1), :].rearrange("(m r) h -> m r h", r=4)
            nc.sync.dma_start(out=dst[:, r0:r1, :], in_=o1_t[g][:, r0:r1, :])

        load_s(0, 0, 1)
        act(0, ACT.Tanh, 0, 1)
        act(0, ACT.Square, 0, 1)
        load_d(0)
        make_d2(0)
        load_s(0, 3, 4)
        act(0, ACT.Tanh, 3, 4)
        load_s(0, 1, 2)
        act(0, ACT.Tanh, 1, 2)
        act(0, ACT.Square, 1, 2)
        act(0, ACT.Square, 3, 4)
        load_g(0, 0, 512)
        stt(0, 0, 1)
        load_s(0, 2, 3)
        act(0, ACT.Tanh, 2, 3)
        act(0, ACT.Square, 2, 3)
        stt(0, 1, 2)
        tr(0, 0)
        cp(0, 0, "s")
        load_s(1)
        act(1, ACT.Tanh, 2, 4)
        q_d(0)
        stt(0, 3, 4)
        stt(0, 2, 3)
        tr(0, 1)
        il(0, 0, 4, "v")
        load_d(1)
        make_d2(1)
        q_t(0)
        q_d(1)
        act(1, ACT.Tanh, 0, 2)
        act(1, ACT.Square, 2, 4)
        load_g(0, 512, 1024)
        act(1, ACT.Square, 0, 2)
        stt(1)
        tr(1, 0)
        cp(0, 1, "s")
        tr(1, 1)
        q_r(0)
        load_s(2)
        act(2, ACT.Tanh, 0, 2)
        act(2, ACT.Tanh, 2, 4)
        act(2, ACT.Square, 0, 2)
        il(1, 1, 4, "v")
        load_z(0)
        load_rz(0)
        make_p(0, 0)
        make_p(0, 1)
        act(2, ACT.Square, 2, 4)
        cp(1, 1, "s")
        cp(1, 0, "s")
        q_r(1)
        mm0(0, 0)
        mm0(0, 1)
        q_p(0)
        il(1, 0, 1, "s")
        q_t(1)
        ev0(0, 0)
        mm0(0, 2)
        load_s(3)
        act(3, ACT.Tanh, 0, 2)
        act(3, ACT.Tanh, 2, 4)
        act(3, ACT.Square, 0, 2)
        load_g(1)
        stt(2)
        tr(2, 0)
        tr(2, 1)
        ev0(0, 1)
        act(3, ACT.Square, 2, 4)
        load_s(4)
        act(4, ACT.Tanh, 0, 2)
        act(4, ACT.Tanh, 2, 4)
        cp(2, 0, "s")
        stt(3)
        il(3, 0, 2, "s")
        act(4, ACT.Square, 0, 2)
        ev0(0, 2)
        il(3, 2, 4, "v")
        cp(2, 1, "s")
        mm0(0, 3)
        ev0(0, 3)
        il(2, 1, 4, "v")
        load_rz(1)
        load_z(1)
        make_p(1, 0)
        q_r(2)
        make_p(1, 1)
        tr(3, 0)
        il(2, 0, 1, "s")
        load_g(2)
        act(4, ACT.Square, 2, 4)
        stt(4)
        q_p(1)
        tr(3, 1)
        cp(3, 1, "s")
        cp(3, 0, "s")
        q_r(3)
        tr(4, 0)
        tr(4, 1)
        load_s(5)
        act(5, ACT.Tanh, 2, 4)
        act(5, ACT.Square, 2, 4)
        act(5, ACT.Tanh, 0, 2)
        act(5, ACT.Square, 0, 2)
        cp(4, 0, "s")
        q_t(3)
        il(4, 0, 2, "s")
        q_t(2)
        cp(4, 1, "s")
        load_rz(2)
        load_z(2)
        make_p(2, 0)
        load_s(6)
        act(6, ACT.Tanh, 0, 2)
        load_s(7)
        act(7, ACT.Tanh, 0, 2)
        mm0(1, 0)
        ev0(1, 0)
        mm0(1, 1)
        mm0(1, 2)
        make_p(2, 1)
        ev0(1, 1)
        stt(5)
        il(4, 2, 4, "v")
        mm0(1, 3)
        q_r(4)
        ev0(1, 2)
        q_p(2)
        mm1(0, 0)
        tr(5, 0)
        mm1(1, 0)
        tr(5, 1)
        q_t(4)
        mm1(2, 0)
        load_z(3)
        load_rz(3)
        make_p(3, 0)
        make_p(3, 1)
        act(6, ACT.Tanh, 2, 4)
        act(6, ACT.Square, 0, 2)
        act(7, ACT.Tanh, 2, 4)
        load_g(3)
        act(6, ACT.Square, 2, 4)
        stt(6)
        cp(5, 0, "s")
        tr(6, 0)
        cp(5, 1, "s")
        tr(6, 1)
        ev0(1, 3)
        q_r(5)
        mm0(2, 0)
        mm0(2, 1)
        act(7, ACT.Square, 2, 4)
        il(5, 3, 4, "v")
        act(7, ACT.Square, 0, 2)
        stt(7)
        il(6, 0, 4, "s")
        q_t(6)
        cp(6, 0, "s")
        tr(7, 0)
        cp(6, 1, "s")
        tr(7, 1)
        cp(7, 1, "s")
        q_p(3)
        mm1(3, 0)
        st0(0, 0, 4)
        ev0(2, 1)
        ev0(2, 0)
        mm0(2, 2)
        mm0(2, 3)
        q_r(6)
        ev1(0, 0)
        ev1(0, 1)
        ev1(0, 2)
        st0(1, 0, 4)
        ev1(0, 3)
        st1(0, 0, 4)
        mm1(0, 1)
        cp(7, 0, "s")
        q_r(7)
        il(5, 0, 3, "s")
        q_t(5)
        ev0(2, 2)
        ev0(2, 3)
        st0(2, 0, 4)
        il(7, 2, 4, "v")
        il(7, 0, 2, "s")
        mm0(3, 0, spare=True)
        mm0(3, 1, spare=True)
        ev0(3, 1)
        q_t(7)
        ev0(3, 0)
        st0(3, 0, 2)
        mm1(1, 1)
        mm1(2, 1)
        mm1(3, 1)
        ev1(1, 0)
        ev1(1, 1)
        st1(1, 0, 2)
        ev1(1, 3)
        ev1(1, 2)
        st1(1, 2, 4)
        mm0(3, 2)
        ev0(3, 2)
        st0(3, 2, 3)
        mm0(3, 3)
        ev0(3, 3)
        st0(3, 3, 4)
